import numpy as np
import ml_dtypes


def mxq(x, axis, fmt="e4m3"):
    dtype, down = {"e4m3": (ml_dtypes.float8_e4m3fn, 7), "e5m2": (ml_dtypes.float8_e5m2, 14)}[fmt]
    v = np.moveaxis(np.asarray(x, np.float32).astype(ml_dtypes.bfloat16).astype(np.float64), axis, -1)
    blocks = v.reshape(v.shape[:-1] + (-1, 32))
    amax = np.abs(blocks).max(-1, keepdims=True)
    byte = np.maximum(np.where(amax > 0, np.frexp(amax)[1] - 1 + 127, 0) - down, 1)
    scale = np.exp2(byte - 127.0)
    codes = (blocks / scale).astype(np.float32).astype(dtype).astype(np.float64)
    return np.moveaxis((codes * scale).reshape(v.shape), -1, axis)


WIDE = False


def mx_kscale(k):
    if not WIDE:
        return np.ones(k)
    levels = np.array([10, -10, 5, -5, 0])
    a = np.random.permutation(np.resize(levels, k // 512 * 4)).reshape(k // 512, 4)
    idx = np.arange(k)
    return np.exp2(a[idx // 512, idx % 128 // 32])


BF16 = ml_dtypes.bfloat16


def bf(x):
    return np.asarray(x, np.float32).astype(BF16)


def f64(x):
    return np.asarray(x).astype(np.float64)


B, S, HID, NH, NKV, HD, FF = 16, 512, 512, 1, 1, 128, 8192
T = B * S
EPS = 1e-6


def rms(u, w):
    return u * (1.0 / np.sqrt(np.mean(u * u, axis=-1, keepdims=True) + EPS)) * w


def rotate_half(u):
    u1, u2 = np.split(u, 2, axis=-1)
    return np.concatenate([-u2, u1], axis=-1)


def setup_inputs():
    s = mx_kscale(HID)
    pos = np.tile(np.arange(S, dtype=np.float64), B)
    inv_freq = 1.0 / (10000.0 ** (np.arange(0, HD, 2, dtype=np.float64) / HD))
    ang = pos[:, None] * inv_freq[None, :]
    emb = np.concatenate([ang, ang], axis=-1)
    a = 1.0 / np.sqrt(HID)
    return {"x": bf(np.random.standard_normal((T, HID)) * 0.5),
            "cos": bf(np.cos(emb)),
            "sin": bf(np.sin(emb)),
            "wq": bf(np.random.standard_normal((NH * HD, HID)) * a / s[None, :]),
            "bq": bf(np.random.standard_normal(NH * HD) * 0.3),
            "wk": bf(np.random.standard_normal((NKV * HD, HID)) * a / s[None, :]),
            "bk": bf(np.random.standard_normal(NKV * HD) * 0.3),
            "wv": bf(np.random.standard_normal((NKV * HD, HID)) * 2.0 * a / s[None, :]),
            "bv": bf(np.random.standard_normal(NKV * HD) * 0.3),
            "q_norm_w": bf(1.0 + 0.1 * np.random.standard_normal(HD)),
            "k_norm_w": bf(1.0 + 0.1 * np.random.standard_normal(HD)),
            "ln1_w": bf((1.0 + 0.1 * np.random.standard_normal(HID)) * s)}


def reference(x, cos, sin, wq, bq, wk, bk, wv, bv, q_norm_w, k_norm_w, ln1_w):
    h = rms(f64(x), f64(ln1_w))
    hq = mxq(h, 1, "e4m3")
    q = ((hq @ mxq(f64(wq), 1, "e4m3").T) + f64(bq)).reshape(T, NH, HD)
    k = ((hq @ mxq(f64(wk), 1, "e4m3").T) + f64(bk)).reshape(T, NKV, HD)
    v = ((hq @ mxq(f64(wv), 1, "e4m3").T) + f64(bv)).reshape(T, NKV, HD)
    q = rms(q, f64(q_norm_w))
    k = rms(k, f64(k_norm_w))
    c, sn = f64(cos)[:, None, :], f64(sin)[:, None, :]
    q = q * c + rotate_half(q) * sn
    k = k * c + rotate_half(k) * sn
    return q, k, v

@@ -1,0 +1,326 @@
+from contextlib import ExitStack
+
+import concourse.mybir as mybir
+from concourse.masks import make_identity
+
+F32 = mybir.dt.float32
+BF16 = mybir.dt.bfloat16
+U32 = mybir.dt.uint32
+U8 = mybir.dt.uint8
+FP8X4 = mybir.dt.float8_e4m3fn_x4
+ALU = mybir.AluOpType
+ACT = mybir.ActivationFunctionType
+
+P = 128
+TOKENS = 8192
+HID = 512
+HD = 128
+HALF = HD // 2
+EPS = 1e-6
+TILES = 2
+UNIT = TILES * P
+N_UNITS = TOKENS // UNIT
+DEPTH = 6
+WEIGHTS_ROUND = 2
+
+FLOPS = 2 * TOKENS * HID * 3 * HD
+
+
+def tile_qwen2decoderlayer_pa_t_kernel(
+    tc, x, cos, sin, wq, bq, wk, bk, wv, bv, q_norm_w, k_norm_w, ln1_w, out_0, out_1, out_2
+):
+    nc = tc.nc
+    q_out = out_0.flatten_outer_dims()
+    k_out = out_1.flatten_outer_dims()
+    v_out = out_2.flatten_outer_dims()
+
+    with ExitStack() as ctx:
+        ctx.enter_context(tc.manual_schedule())
+        consts = ctx.enter_context(tc.tile_pool(name="consts", bufs=1))
+        inputs = ctx.enter_context(tc.tile_pool(name="inputs", bufs=N_UNITS))
+        work = ctx.enter_context(tc.tile_pool(name="work", bufs=3))
+        small = ctx.enter_context(tc.tile_pool(name="small", bufs=4))
+        unread = ctx.enter_context(tc.tile_pool(name="unread", bufs=4))
+        results = ctx.enter_context(tc.tile_pool(name="results", bufs=6))
+        psum = ctx.enter_context(tc.psum_pool(name="psum", bufs=2))
+
+        x_of, cos_of, sin_of = {}, {}, {}
+
+        def load_x(u):
+            x_sb = inputs.tile([P, TILES, HID], BF16)
+            nc.sync.dma_start(
+                out=x_sb[:],
+                in_=x[u * UNIT : (u + 1) * UNIT, :].rearrange("(p j) k -> p j k", j=TILES),
+            )
+            x_of[u] = x_sb
+
+        def load_angles(u):
+            rows = slice(u * UNIT, (u + 1) * UNIT)
+            cos_sb = inputs.tile([P, TILES, HD], BF16)
+            nc.sync.dma_start(
+                out=cos_sb[:], in_=cos[rows, :].rearrange("(p j) d -> p j d", j=TILES)
+            )
+            sin_sb = inputs.tile([P, TILES, HD], BF16)
+            nc.sync.dma_start(
+                out=sin_sb[:], in_=sin[rows, :].rearrange("(p j) d -> p j d", j=TILES)
+            )
+            cos_of[u], sin_of[u] = cos_sb, sin_sb
+
+        load_x(0)
+        ln1_gain = consts.tile([P, HID], BF16)
+        nc.sync.dma_start(out=ln1_gain[:], in_=ln1_w.partition_broadcast(P))
+        load_x(1)
+        w_rows = consts.tile([P, 3, HID], BF16)
+        for head, w in enumerate((wq, wk, wv)):
+            nc.sync.dma_start(out=w_rows[:, head, :], in_=w)
+        load_x(2)
+        bias_rows = consts.tile([P, P], BF16)
+        nc.vector.memset(bias_rows[:], 0.0)
+        for head, b in enumerate((bq, bk, bv)):
+            nc.sync.dma_start(
+                out=bias_rows[head : head + 1, :], in_=b.rearrange("(o d) -> o d", o=1)
+            )
+        head_gain = consts.tile([P, 2, HD], BF16)
+        for head, g in enumerate((q_norm_w, k_norm_w)):
+            nc.sync.dma_start(out=head_gain[:, head, :], in_=g.partition_broadcast(P))
+        for u in range(N_UNITS):
+            if u + 3 < N_UNITS:
+                load_x(u + 3)
+            load_angles(u)
+
+        eps_col = consts.tile([P, 1], F32)
+        nc.vector.memset(eps_col[:], EPS)
+        first_sqrt = consts.tile([P, 1], F32)
+        nc.scalar.activation(out=first_sqrt[:], in_=eps_col[:], func=ACT.Sqrt)
+        ident_f32 = consts.tile([P, P], F32)
+        make_identity(nc, ident_f32[:])
+        ident_bf16 = consts.tile([P, P], BF16)
+        make_identity(nc, ident_bf16[:])
+
+        w_grouped = consts.tile([P, 3, HID], BF16, align_bytes=64)
+        w_codes = consts.tile([P, 3 * HD], U32, align_bytes=64)
+        w_scales = consts.tile([P, 3 * HD], U8, align_bytes=64)
+        bias_col = consts.tile([P, 3], F32)
+
+        def prepare_weights():
+            for head in range(3):
+                wT_ps = psum.tile([P, 2, HD], F32, tag="back_qk")
+                for half in range(2):
+                    nc.tensor.transpose(
+                        wT_ps[:, half, :],
+                        w_rows[:, head, :].bitcast(F32)[:, half * P : (half + 1) * P],
+                        ident_f32[:],
+                    )
+                nc.vector.tensor_copy(
+                    out=w_grouped[:, head, :].bitcast(F32).rearrange("p (d h) -> p d h", h=2),
+                    in_=wT_ps[:].rearrange("p h d -> p d h"),
+                )
+            for head in range(3):
+                cols = slice(head * HD, (head + 1) * HD)
+                nc.vector.quantize_mx(
+                    out=w_codes[:, cols].bitcast(FP8X4),
+                    scales=w_scales[:, cols],
+                    in_=w_grouped[:, head, :],
+                )
+            biasT_ps = psum.tile([P, P], BF16, tag="back_qk")
+            nc.tensor.transpose(biasT_ps[:], bias_rows[:], ident_bf16[:])
+            nc.vector.tensor_copy(out=bias_col[:], in_=biasT_ps[:, 0:3])
+
+        x_ss_of, x_std_of, x_rstd_of, h_of, hT_of, grouped_of = {}, {}, {}, {}, {}, {}
+        codes_of, scales_of, acc_qk_of, v_ps_of, t1T_of, back_of = {}, {}, {}, {}, {}, {}
+        head_std_of, head_rstd_of, normed_of = {}, {}, {}
+
+        def x_sum_of_squares(u):
+            x_ss = small.tile([P, TILES], F32)
+            for j in range(TILES):
+                x_sq = unread.tile([P, HID], BF16)
+                nc.scalar.activation(
+                    out=x_sq[:], in_=x_of[u][:, j, :], func=ACT.Square,
+                    accum_out=x_ss[:, j : j + 1],
+                )
+            x_ss_of[u] = x_ss
+
+        def x_std(u):
+            std = small.tile([P, TILES], F32, name="x_std_sb")
+            nc.scalar.activation(
+                out=std[:], in_=x_ss_of[u][:], func=ACT.Sqrt, bias=eps_col[:], scale=1.0 / HID
+            )
+            x_std_of[u] = std
+
+        def x_rstd(u):
+            rstd = small.tile([P, TILES], F32, name="x_rstd_sb")
+            nc.vector.reciprocal(out=rstd[:], in_=x_std_of[u][:])
+            x_rstd_of[u] = rstd
+
+        def first_norm(u):
+            h_sb = work.tile([P, TILES, HID], BF16)
+            for j in range(TILES):
+                nc.vector.scalar_tensor_tensor(
+                    out=h_sb[:, j, :], in0=x_of[u][:, j, :], scalar=x_rstd_of[u][:, j : j + 1],
+                    in1=ln1_gain[:], op0=ALU.mult, op1=ALU.mult,
+                )
+            h_of[u] = h_sb
+
+        def h_transposes(u):
+            hT_ps = psum.tile([P, TILES, 2, P], F32)
+            for j in range(TILES):
+                for half in range(2):
+                    nc.tensor.transpose(
+                        hT_ps[:, j, half, :],
+                        h_of[u][:, j, :].bitcast(F32)[:, half * P : (half + 1) * P],
+                        ident_f32[:],
+                    )
+            hT_of[u] = hT_ps
+
+        def h_regroup(u):
+            h_grouped = work.tile([P, UNIT * 4], BF16, align_bytes=64)
+            nc.scalar.copy(
+                out=h_grouped[:].bitcast(F32).rearrange("p (j t h) -> p j t h", j=TILES, h=2),
+                in_=hT_of[u][:].rearrange("p j h t -> p j t h"),
+            )
+            grouped_of[u] = h_grouped
+
+        def h_quantise(u):
+            h_codes = work.tile([P, UNIT], U32, align_bytes=64)
+            h_scales = work.tile([P, UNIT], U8, align_bytes=64)
+            nc.vector.quantize_mx(
+                out=h_codes[:].bitcast(FP8X4), scales=h_scales[:], in_=grouped_of[u][:]
+            )
+            codes_of[u], scales_of[u] = h_codes, h_scales
+
+        def projections(u):
+            acc_qk = psum.tile([P, 2, UNIT], F32)
+            v_ps = psum.tile([P, 2 * UNIT], F32)
+            for head, acc in enumerate((acc_qk[:, 0, :], acc_qk[:, 1, :], v_ps[:, 0:UNIT])):
+                cols = slice(head * HD, (head + 1) * HD)
+                nc.tensor.matmul_mx(
+                    out=acc,
+                    lhsT=w_codes[:, cols].bitcast(FP8X4), lhsT_scale=w_scales[:, cols],
+                    rhs=codes_of[u][:].bitcast(FP8X4), rhs_scale=scales_of[u][:],
+                    start=True, stop=True,
+                )
+            acc_qk_of[u], v_ps_of[u] = acc_qk, v_ps
+
+        def add_biases(u):
+            t1T = work.tile([P, 3, UNIT], F32)
+            accs = (acc_qk_of[u][:, 0, :], acc_qk_of[u][:, 1, :], v_ps_of[u][:, 0:UNIT])
+            for head, acc in enumerate(accs):
+                nc.scalar.activation(
+                    out=t1T[:, head, :], in_=acc, func=ACT.Identity,
+                    bias=bias_col[:, head : head + 1],
+                )
+            t1T_of[u] = t1T
+
+        def turn_back(u):
+            back_qk = psum.tile([P, 2, TILES, HD], F32)
+            for j in range(TILES):
+                tok = slice(j * P, (j + 1) * P)
+                for head in range(2):
+                    nc.tensor.transpose(back_qk[:, head, j, :], t1T_of[u][:, head, tok], ident_f32[:])
+                nc.tensor.transpose(
+                    v_ps_of[u][:, UNIT + j * HD : UNIT + (j + 1) * HD], t1T_of[u][:, 2, tok],
+                    ident_f32[:],
+                )
+            back_of[u] = back_qk
+
+        def head_statistics(u):
+            head_ss = small.tile([P, 2, TILES], F32)
+            for head in range(2):
+                for j in range(TILES):
+                    head_sq = unread.tile([P, HD], BF16)
+                    nc.scalar.activation(
+                        out=head_sq[:], in_=back_of[u][:, head, j, :], func=ACT.Square,
+                        accum_out=head_ss[:, head, j : j + 1],
+                    )
+            v_sb = results.tile([P, TILES, HD], F32)
+            nc.scalar.copy(
+                out=v_sb[:],
+                in_=v_ps_of[u][:, UNIT : 2 * UNIT].rearrange("p (j d) -> p j d", j=TILES),
+            )
+            rows = slice(u * UNIT, (u + 1) * UNIT)
+            nc.sync.dma_start(
+                out=v_out[rows, :].rearrange("(p j) d -> p j d", j=TILES), in_=v_sb[:]
+            )
+            head_std = small.tile([P, 2, TILES], F32)
+            nc.scalar.activation(
+                out=head_std[:], in_=head_ss[:], func=ACT.Sqrt, bias=eps_col[:], scale=1.0 / HD
+            )
+            head_std_of[u] = head_std
+
+        def head_rstd(u):
+            rstd = small.tile([P, 2, TILES], F32, name="head_rstd_sb")
+            nc.vector.reciprocal(out=rstd[:], in_=head_std_of[u][:])
+            head_rstd_of[u] = rstd
+
+        def head_norm(u):
+            normed = work.tile([P, 2, TILES, HD], F32)
+            for head in range(2):
+                for j in range(TILES):
+                    nc.vector.scalar_tensor_tensor(
+                        out=normed[:, head, j, :], in0=back_of[u][:, head, j, :],
+                        scalar=head_rstd_of[u][:, head, j : j + 1], in1=head_gain[:, head, :],
+                        op0=ALU.mult, op1=ALU.mult,
+                    )
+            normed_of[u] = normed
+
+        def rope(u):
+            normed = normed_of[u]
+            lo, hi = slice(0, HALF), slice(HALF, HD)
+            both = [P, 2, TILES, HD]
+            both_half = [P, 2, TILES, HALF]
+            direct = work.tile(both, F32)
+            nc.vector.tensor_tensor(
+                out=direct[:], in0=normed[:], in1=cos_of[u][:].unsqueeze(1).to_broadcast(both),
+                op=ALU.mult,
+            )
+            crossed = work.tile(both, F32)
+            for here, there in ((lo, hi), (hi, lo)):
+                nc.vector.tensor_tensor(
+                    out=crossed[:, :, :, here], in0=normed[:, :, :, there],
+                    in1=sin_of[u][:, :, here].unsqueeze(1).to_broadcast(both_half), op=ALU.mult,
+                )
+            qk_sb = results.tile(both, F32)
+            for here, op in ((lo, ALU.subtract), (hi, ALU.add)):
+                nc.vector.tensor_tensor(
+                    out=qk_sb[:, :, :, here], in0=direct[:, :, :, here],
+                    in1=crossed[:, :, :, here], op=op,
+                )
+            rows = slice(u * UNIT, (u + 1) * UNIT)
+            for head, out in enumerate((q_out, k_out)):
+                nc.sync.dma_start(
+                    out=out[rows, :].rearrange("(p j) d -> p j d", j=TILES),
+                    in_=qk_sb[:, head, :, :],
+                )
+
+        def live(u):
+            return 0 <= u < N_UNITS
+
+        for r in range(N_UNITS + DEPTH):
+            if r == WEIGHTS_ROUND:
+                prepare_weights()
+            if live(r - 1):
+                x_std(r - 1)
+            if live(r - 5):
+                head_statistics(r - 5)
+            if live(r - 6):
+                rope(r - 6)
+            if live(r - 5):
+                head_rstd(r - 5)
+            if live(r - 1):
+                x_rstd(r - 1)
+            if live(r - 3):
+                h_quantise(r - 3)
+            if live(r - 4):
+                add_biases(r - 4)
+                turn_back(r - 4)
+            if live(r - 3):
+                projections(r - 3)
+            if live(r - 5):
+                head_norm(r - 5)
+            if live(r - 2):
+                h_regroup(r - 2)
+            if live(r):
+                x_sum_of_squares(r)
+            if live(r - 1):
+                first_norm(r - 1)
+                h_transposes(r - 1)

@@ -298,29 +298,28 @@ def tile_qwen2decoderlayer_pa_t_kernel(
         for r in range(N_UNITS + DEPTH):
             if r == WEIGHTS_ROUND:
                 prepare_weights()
-            if live(r - 1):
-                x_std(r - 1)
             if live(r - 5):
                 head_statistics(r - 5)
-            if live(r - 6):
-                rope(r - 6)
-            if live(r - 5):
-                head_rstd(r - 5)
             if live(r - 1):
                 x_rstd(r - 1)
             if live(r - 3):
                 h_quantise(r - 3)
+                projections(r - 3)
+            if live(r - 6):
+                rope(r - 6)
             if live(r - 4):
                 add_biases(r - 4)
                 turn_back(r - 4)
-            if live(r - 3):
-                projections(r - 3)
             if live(r - 5):
-                head_norm(r - 5)
+                head_rstd(r - 5)
+            if live(r):
+                x_sum_of_squares(r)
             if live(r - 2):
                 h_regroup(r - 2)
             if live(r):
-                x_sum_of_squares(r)
+                x_std(r)
             if live(r - 1):
                 first_norm(r - 1)
                 h_transposes(r - 1)
+            if live(r - 5):
+                head_norm(r - 5)

@@ -22,6 +22,8 @@ UNIT = TILES * P
 N_UNITS = TOKENS // UNIT
 DEPTH = 6
 WEIGHTS_ROUND = 2
+GAIN_ROWS = HID // P
+VECTOR_SHARE = 4
 
 FLOPS = 2 * TOKENS * HID * 3 * HD
 
@@ -67,19 +69,21 @@ def tile_qwen2decoderlayer_pa_t_kernel(
             cos_of[u], sin_of[u] = cos_sb, sin_sb
 
         load_x(0)
-        ln1_gain = consts.tile([P, HID], BF16)
-        nc.sync.dma_start(out=ln1_gain[:], in_=ln1_w.partition_broadcast(P))
+        vector_rows = consts.tile([P, P], BF16)
+        nc.vector.memset(vector_rows[:], 0.0)
+        nc.sync.dma_start(
+            out=vector_rows[0:GAIN_ROWS, :], in_=ln1_w.rearrange("(c k) -> c k", c=GAIN_ROWS)
+        )
+        for head, b in enumerate((bq, bk, bv)):
+            nc.sync.dma_start(
+                out=vector_rows[GAIN_ROWS + head : GAIN_ROWS + head + 1, :],
+                in_=b.rearrange("(o d) -> o d", o=1),
+            )
         load_x(1)
         w_rows = consts.tile([P, 3, HID], BF16)
         for head, w in enumerate((wq, wk, wv)):
             nc.sync.dma_start(out=w_rows[:, head, :], in_=w)
         load_x(2)
-        bias_rows = consts.tile([P, P], BF16)
-        nc.vector.memset(bias_rows[:], 0.0)
-        for head, b in enumerate((bq, bk, bv)):
-            nc.sync.dma_start(
-                out=bias_rows[head : head + 1, :], in_=b.rearrange("(o d) -> o d", o=1)
-            )
         head_gain = consts.tile([P, 2, HD], BF16)
         for head, g in enumerate((q_norm_w, k_norm_w)):
             nc.sync.dma_start(out=head_gain[:, head, :], in_=g.partition_broadcast(P))
@@ -97,10 +101,22 @@ def tile_qwen2decoderlayer_pa_t_kernel(
         ident_bf16 = consts.tile([P, P], BF16)
         make_identity(nc, ident_bf16[:])
 
+        vectorsT_ps = psum.tile([P, P], BF16, tag="back_qk")
+        nc.tensor.transpose(vectorsT_ps[:], vector_rows[:], ident_bf16[:])
+        vector_cols = consts.tile([P, GAIN_ROWS + 3], F32)
+        nc.vector.tensor_copy(out=vector_cols[:], in_=vectorsT_ps[:, 0 : GAIN_ROWS + 3])
+        bias_col = vector_cols[:, GAIN_ROWS : GAIN_ROWS + 3]
+        ln1_gain = psum.tile([P, HID], F32, bufs=1)
+        for c in range(GAIN_ROWS):
+            nc.tensor.transpose(
+                ln1_gain[:, c * P : (c + 1) * P],
+                vector_cols[:, c : c + 1].to_broadcast([P, P]),
+                ident_f32[:],
+            )
+
         w_grouped = consts.tile([P, 3, HID], BF16, align_bytes=64)
         w_codes = consts.tile([P, 3 * HD], U32, align_bytes=64)
         w_scales = consts.tile([P, 3 * HD], U8, align_bytes=64)
-        bias_col = consts.tile([P, 3], F32)
 
         def prepare_weights():
             for head in range(3):
@@ -122,9 +138,6 @@ def tile_qwen2decoderlayer_pa_t_kernel(
                     scales=w_scales[:, cols],
                     in_=w_grouped[:, head, :],
                 )
-            biasT_ps = psum.tile([P, P], BF16, tag="back_qk")
-            nc.tensor.transpose(biasT_ps[:], bias_rows[:], ident_bf16[:])
-            nc.vector.tensor_copy(out=bias_col[:], in_=biasT_ps[:, 0:3])
 
         x_ss_of, x_std_of, x_rstd_of, h_of, hT_of, grouped_of = {}, {}, {}, {}, {}, {}
         codes_of, scales_of, acc_qk_of, v_ps_of, t1T_of, back_of = {}, {}, {}, {}, {}, {}
@@ -162,7 +175,7 @@ def tile_qwen2decoderlayer_pa_t_kernel(
             h_of[u] = h_sb
 
         def h_transposes(u):
-            hT_ps = psum.tile([P, TILES, 2, P], F32)
+            hT_ps = psum.tile([P, TILES, 2, P], F32, bufs=1)
             for j in range(TILES):
                 for half in range(2):
                     nc.tensor.transpose(
@@ -174,10 +187,14 @@ def tile_qwen2decoderlayer_pa_t_kernel(
 
         def h_regroup(u):
             h_grouped = work.tile([P, UNIT * 4], BF16, align_bytes=64)
-            nc.scalar.copy(
-                out=h_grouped[:].bitcast(F32).rearrange("p (j t h) -> p j t h", j=TILES, h=2),
-                in_=hT_of[u][:].rearrange("p j h t -> p j t h"),
+            side_by_side = h_grouped[:].bitcast(F32).rearrange(
+                "p (j t h) -> p j t h", j=TILES, h=2
             )
+            by_half = hT_of[u][:].rearrange("p j h t -> p j t h")
+            if u % VECTOR_SHARE == 0:
+                nc.vector.tensor_copy(out=side_by_side, in_=by_half)
+            else:
+                nc.scalar.copy(out=side_by_side, in_=by_half)
             grouped_of[u] = h_grouped
 
         def h_quantise(u):
@@ -281,7 +298,7 @@ def tile_qwen2decoderlayer_pa_t_kernel(
                 )
             qk_sb = results.tile(both, F32)
             for here, op in ((lo, ALU.subtract), (hi, ALU.add)):
-                nc.vector.tensor_tensor(
+                nc.gpsimd.tensor_tensor(
                     out=qk_sb[:, :, :, here], in0=direct[:, :, :, here],
                     in1=crossed[:, :, :, here], op=op,
                 )

@@ -23,7 +23,6 @@ N_UNITS = TOKENS // UNIT
 DEPTH = 6
 WEIGHTS_ROUND = 2
 GAIN_ROWS = HID // P
-VECTOR_SHARE = 4
 
 FLOPS = 2 * TOKENS * HID * 3 * HD
 
@@ -74,7 +73,7 @@ def tile_qwen2decoderlayer_pa_t_kernel(
         nc.sync.dma_start(
             out=vector_rows[0:GAIN_ROWS, :], in_=ln1_w.rearrange("(c k) -> c k", c=GAIN_ROWS)
         )
-        for head, b in enumerate((bq, bk, bv)):
+        for head, b in enumerate((bq, bk)):
             nc.sync.dma_start(
                 out=vector_rows[GAIN_ROWS + head : GAIN_ROWS + head + 1, :],
                 in_=b.rearrange("(o d) -> o d", o=1),
@@ -84,6 +83,8 @@ def tile_qwen2decoderlayer_pa_t_kernel(
         for head, w in enumerate((wq, wk, wv)):
             nc.sync.dma_start(out=w_rows[:, head, :], in_=w)
         load_x(2)
+        v_bias = consts.tile([P, HD], BF16)
+        nc.sync.dma_start(out=v_bias[:], in_=bv.partition_broadcast(P))
         head_gain = consts.tile([P, 2, HD], BF16)
         for head, g in enumerate((q_norm_w, k_norm_w)):
             nc.sync.dma_start(out=head_gain[:, head, :], in_=g.partition_broadcast(P))
@@ -103,9 +104,9 @@ def tile_qwen2decoderlayer_pa_t_kernel(
 
         vectorsT_ps = psum.tile([P, P], BF16, tag="back_qk")
         nc.tensor.transpose(vectorsT_ps[:], vector_rows[:], ident_bf16[:])
-        vector_cols = consts.tile([P, GAIN_ROWS + 3], F32)
-        nc.vector.tensor_copy(out=vector_cols[:], in_=vectorsT_ps[:, 0 : GAIN_ROWS + 3])
-        bias_col = vector_cols[:, GAIN_ROWS : GAIN_ROWS + 3]
+        vector_cols = consts.tile([P, GAIN_ROWS + 2], F32)
+        nc.vector.tensor_copy(out=vector_cols[:], in_=vectorsT_ps[:, 0 : GAIN_ROWS + 2])
+        bias_col = vector_cols[:, GAIN_ROWS : GAIN_ROWS + 2]
         ln1_gain = psum.tile([P, HID], F32, bufs=1)
         for c in range(GAIN_ROWS):
             nc.tensor.transpose(
@@ -141,7 +142,7 @@ def tile_qwen2decoderlayer_pa_t_kernel(
 
         x_ss_of, x_std_of, x_rstd_of, h_of, hT_of, grouped_of = {}, {}, {}, {}, {}, {}
         codes_of, scales_of, acc_qk_of, v_ps_of, t1T_of, back_of = {}, {}, {}, {}, {}, {}
-        head_std_of, head_rstd_of, normed_of = {}, {}, {}
+        head_ss_of, head_std_of, head_rstd_of, normed_of = {}, {}, {}, {}
 
         def x_sum_of_squares(u):
             x_ss = small.tile([P, TILES], F32)
@@ -187,14 +188,10 @@ def tile_qwen2decoderlayer_pa_t_kernel(
 
         def h_regroup(u):
             h_grouped = work.tile([P, UNIT * 4], BF16, align_bytes=64)
-            side_by_side = h_grouped[:].bitcast(F32).rearrange(
-                "p (j t h) -> p j t h", j=TILES, h=2
+            nc.scalar.copy(
+                out=h_grouped[:].bitcast(F32).rearrange("p (j t h) -> p j t h", j=TILES, h=2),
+                in_=hT_of[u][:].rearrange("p j h t -> p j t h"),
             )
-            by_half = hT_of[u][:].rearrange("p j h t -> p j t h")
-            if u % VECTOR_SHARE == 0:
-                nc.vector.tensor_copy(out=side_by_side, in_=by_half)
-            else:
-                nc.scalar.copy(out=side_by_side, in_=by_half)
             grouped_of[u] = h_grouped
 
         def h_quantise(u):
@@ -207,40 +204,57 @@ def tile_qwen2decoderlayer_pa_t_kernel(
 
         def projections(u):
             acc_qk = psum.tile([P, 2, UNIT], F32)
-            v_ps = psum.tile([P, 2 * UNIT], F32)
-            for head, acc in enumerate((acc_qk[:, 0, :], acc_qk[:, 1, :], v_ps[:, 0:UNIT])):
+            for head in range(2):
                 cols = slice(head * HD, (head + 1) * HD)
                 nc.tensor.matmul_mx(
-                    out=acc,
+                    out=acc_qk[:, head, :],
                     lhsT=w_codes[:, cols].bitcast(FP8X4), lhsT_scale=w_scales[:, cols],
                     rhs=codes_of[u][:].bitcast(FP8X4), rhs_scale=scales_of[u][:],
                     start=True, stop=True,
                 )
+            v_ps = psum.tile([P, TILES, HD], F32)
+            v_cols = slice(2 * HD, 3 * HD)
+            for j in range(TILES):
+                tok = slice(j * P, (j + 1) * P)
+                nc.tensor.matmul_mx(
+                    out=v_ps[:, j, :],
+                    lhsT=codes_of[u][:, tok].bitcast(FP8X4), lhsT_scale=scales_of[u][:, tok],
+                    rhs=w_codes[:, v_cols].bitcast(FP8X4), rhs_scale=w_scales[:, v_cols],
+                    start=True, stop=True,
+                )
             acc_qk_of[u], v_ps_of[u] = acc_qk, v_ps
 
+        def finish_v(u):
+            v_sb = results.tile([P, TILES, HD], F32)
+            nc.vector.tensor_tensor(
+                out=v_sb[:], in0=v_ps_of[u][:],
+                in1=v_bias[:].unsqueeze(1).to_broadcast([P, TILES, HD]), op=ALU.add,
+            )
+            nc.sync.dma_start(
+                out=v_out[u * UNIT : (u + 1) * UNIT, :].rearrange("(p j) d -> p j d", j=TILES),
+                in_=v_sb[:],
+            )
+
         def add_biases(u):
-            t1T = work.tile([P, 3, UNIT], F32)
-            accs = (acc_qk_of[u][:, 0, :], acc_qk_of[u][:, 1, :], v_ps_of[u][:, 0:UNIT])
-            for head, acc in enumerate(accs):
+            t1T = work.tile([P, 2, UNIT], F32)
+            for head in range(2):
                 nc.scalar.activation(
-                    out=t1T[:, head, :], in_=acc, func=ACT.Identity,
+                    out=t1T[:, head, :], in_=acc_qk_of[u][:, head, :], func=ACT.Identity,
                     bias=bias_col[:, head : head + 1],
                 )
             t1T_of[u] = t1T
 
         def turn_back(u):
             back_qk = psum.tile([P, 2, TILES, HD], F32)
-            for j in range(TILES):
-                tok = slice(j * P, (j + 1) * P)
-                for head in range(2):
-                    nc.tensor.transpose(back_qk[:, head, j, :], t1T_of[u][:, head, tok], ident_f32[:])
-                nc.tensor.transpose(
-                    v_ps_of[u][:, UNIT + j * HD : UNIT + (j + 1) * HD], t1T_of[u][:, 2, tok],
-                    ident_f32[:],
-                )
+            for head in range(2):
+                for j in range(TILES):
+                    nc.tensor.transpose(
+                        back_qk[:, head, j, :], t1T_of[u][:, head, j * P : (j + 1) * P],
+                        ident_f32[:],
+                    )
             back_of[u] = back_qk
 
-        def head_statistics(u):
+        def head_sums_of_squares(u):
             head_ss = small.tile([P, 2, TILES], F32)
             for head in range(2):
                 for j in range(TILES):
@@ -249,20 +263,14 @@ def tile_qwen2decoderlayer_pa_t_kernel(
                         out=head_sq[:], in_=back_of[u][:, head, j, :], func=ACT.Square,
                         accum_out=head_ss[:, head, j : j + 1],
                     )
-            v_sb = results.tile([P, TILES, HD], F32)
-            nc.scalar.copy(
-                out=v_sb[:],
-                in_=v_ps_of[u][:, UNIT : 2 * UNIT].rearrange("p (j d) -> p j d", j=TILES),
-            )
-            rows = slice(u * UNIT, (u + 1) * UNIT)
-            nc.sync.dma_start(
-                out=v_out[rows, :].rearrange("(p j) d -> p j d", j=TILES), in_=v_sb[:]
-            )
-            head_std = small.tile([P, 2, TILES], F32)
+            head_ss_of[u] = head_ss
+
+        def head_std(u):
+            std = small.tile([P, 2, TILES], F32, name="head_std_sb")
             nc.scalar.activation(
-                out=head_std[:], in_=head_ss[:], func=ACT.Sqrt, bias=eps_col[:], scale=1.0 / HD
+                out=std[:], in_=head_ss_of[u][:], func=ACT.Sqrt, bias=eps_col[:], scale=1.0 / HD
             )
-            head_std_of[u] = head_std
+            head_std_of[u] = std
 
         def head_rstd(u):
             rstd = small.tile([P, 2, TILES], F32, name="head_rstd_sb")
@@ -316,7 +324,7 @@ def tile_qwen2decoderlayer_pa_t_kernel(
             if r == WEIGHTS_ROUND:
                 prepare_weights()
             if live(r - 5):
-                head_statistics(r - 5)
+                head_sums_of_squares(r - 5)
             if live(r - 1):
                 x_rstd(r - 1)
             if live(r - 3):
@@ -327,7 +335,9 @@ def tile_qwen2decoderlayer_pa_t_kernel(
             if live(r - 4):
                 add_biases(r - 4)
                 turn_back(r - 4)
+                finish_v(r - 4)
             if live(r - 5):
+                head_std(r - 5)
                 head_rstd(r - 5)
             if live(r):
                 x_sum_of_squares(r)

@@ -142,7 +142,7 @@ def tile_qwen2decoderlayer_pa_t_kernel(
 
         x_ss_of, x_std_of, x_rstd_of, h_of, hT_of, grouped_of = {}, {}, {}, {}, {}, {}
         codes_of, scales_of, acc_qk_of, v_ps_of, t1T_of, back_of = {}, {}, {}, {}, {}, {}
-        head_ss_of, head_std_of, head_rstd_of, normed_of = {}, {}, {}, {}
+        head_ss_of, head_std_of, head_rstd_of, normed_of, cos_ps_of = {}, {}, {}, {}, {}
 
         def x_sum_of_squares(u):
             x_ss = small.tile([P, TILES], F32)
@@ -212,7 +212,7 @@ def tile_qwen2decoderlayer_pa_t_kernel(
                     rhs=codes_of[u][:].bitcast(FP8X4), rhs_scale=scales_of[u][:],
                     start=True, stop=True,
                 )
-            v_ps = psum.tile([P, TILES, HD], F32)
+            v_ps = psum.tile([P, TILES, HD], F32, bufs=1)
             v_cols = slice(2 * HD, 3 * HD)
             for j in range(TILES):
                 tok = slice(j * P, (j + 1) * P)
@@ -288,22 +288,29 @@ def tile_qwen2decoderlayer_pa_t_kernel(
                     )
             normed_of[u] = normed
 
+        def cos_to_psum(u):
+            cos_ps = psum.tile([P, TILES, HD], F32, bufs=1)
+            nc.tensor.matmul(
+                out=cos_ps[:], lhsT=ident_bf16[:], rhs=cos_of[u][:], start=True, stop=True
+            )
+            cos_ps_of[u] = cos_ps
+
         def rope(u):
             normed = normed_of[u]
             lo, hi = slice(0, HALF), slice(HALF, HD)
             both = [P, 2, TILES, HD]
             both_half = [P, 2, TILES, HALF]
-            direct = work.tile(both, F32)
-            nc.vector.tensor_tensor(
-                out=direct[:], in0=normed[:], in1=cos_of[u][:].unsqueeze(1).to_broadcast(both),
-                op=ALU.mult,
-            )
             crossed = work.tile(both, F32)
             for here, there in ((lo, hi), (hi, lo)):
-                nc.vector.tensor_tensor(
+                nc.gpsimd.tensor_tensor(
                     out=crossed[:, :, :, here], in0=normed[:, :, :, there],
                     in1=sin_of[u][:, :, here].unsqueeze(1).to_broadcast(both_half), op=ALU.mult,
                 )
+            direct = work.tile(both, F32)
+            nc.vector.tensor_tensor(
+                out=direct[:], in0=cos_ps_of[u][:].unsqueeze(1).to_broadcast(both), in1=normed[:],
+                op=ALU.mult,
+            )
             qk_sb = results.tile(both, F32)
             for here, op in ((lo, ALU.subtract), (hi, ALU.add)):
                 nc.gpsimd.tensor_tensor(
@@ -329,13 +336,17 @@ def tile_qwen2decoderlayer_pa_t_kernel(
                 x_rstd(r - 1)
             if live(r - 3):
                 h_quantise(r - 3)
+            if live(r - 4):
+                finish_v(r - 4)
+            if live(r - 3):
                 projections(r - 3)
             if live(r - 6):
                 rope(r - 6)
+            if live(r - 5):
+                cos_to_psum(r - 5)
             if live(r - 4):
                 add_biases(r - 4)
                 turn_back(r - 4)
-                finish_v(r - 4)
             if live(r - 5):
                 head_std(r - 5)
                 head_rstd(r - 5)

from contextlib import ExitStack

import concourse.mybir as mybir
from concourse.masks import make_identity

F32 = mybir.dt.float32
BF16 = mybir.dt.bfloat16
U32 = mybir.dt.uint32
U8 = mybir.dt.uint8
FP8X4 = mybir.dt.float8_e4m3fn_x4
ALU = mybir.AluOpType
ACT = mybir.ActivationFunctionType

P = 128
TOKENS = 8192
HID = 512
HD = 128
HALF = HD // 2
EPS = 1e-6
TILES = 2
UNIT = TILES * P
N_UNITS = TOKENS // UNIT
DEPTH = 6
WEIGHTS_ROUND = 2
GAIN_ROWS = HID // P

FLOPS = 2 * TOKENS * HID * 3 * HD


def tile_qwen2decoderlayer_pa_t_kernel(
    tc, x, cos, sin, wq, bq, wk, bk, wv, bv, q_norm_w, k_norm_w, ln1_w, out_0, out_1, out_2
):
    nc = tc.nc
    q_out = out_0.flatten_outer_dims()
    k_out = out_1.flatten_outer_dims()
    v_out = out_2.flatten_outer_dims()

    with ExitStack() as ctx:
        ctx.enter_context(tc.manual_schedule())
        consts = ctx.enter_context(tc.tile_pool(name="consts", bufs=1))
        inputs = ctx.enter_context(tc.tile_pool(name="inputs", bufs=N_UNITS))
        work = ctx.enter_context(tc.tile_pool(name="work", bufs=3))
        small = ctx.enter_context(tc.tile_pool(name="small", bufs=4))
        unread = ctx.enter_context(tc.tile_pool(name="unread", bufs=4))
        results = ctx.enter_context(tc.tile_pool(name="results", bufs=6))
        psum = ctx.enter_context(tc.psum_pool(name="psum", bufs=2))

        x_of, cos_of, sin_of = {}, {}, {}

        def load_x(u):
            x_sb = inputs.tile([P, TILES, HID], BF16)
            nc.sync.dma_start(
                out=x_sb[:],
                in_=x[u * UNIT : (u + 1) * UNIT, :].rearrange("(p j) k -> p j k", j=TILES),
            )
            x_of[u] = x_sb

        def load_angles(u):
            rows = slice(u * UNIT, (u + 1) * UNIT)
            cos_sb = inputs.tile([P, TILES, HD], BF16)
            nc.sync.dma_start(
                out=cos_sb[:], in_=cos[rows, :].rearrange("(p j) d -> p j d", j=TILES)
            )
            sin_sb = inputs.tile([P, TILES, HD], BF16)
            nc.sync.dma_start(
                out=sin_sb[:], in_=sin[rows, :].rearrange("(p j) d -> p j d", j=TILES)
            )
            cos_of[u], sin_of[u] = cos_sb, sin_sb

        load_x(0)
        vector_rows = consts.tile([P, P], BF16)
        nc.vector.memset(vector_rows[:], 0.0)
        nc.sync.dma_start(
            out=vector_rows[0:GAIN_ROWS, :], in_=ln1_w.rearrange("(c k) -> c k", c=GAIN_ROWS)
        )
        for head, b in enumerate((bq, bk)):
            nc.sync.dma_start(
                out=vector_rows[GAIN_ROWS + head : GAIN_ROWS + head + 1, :],
                in_=b.rearrange("(o d) -> o d", o=1),
            )
        load_x(1)
        w_rows = consts.tile([P, 3, HID], BF16)
        for head, w in enumerate((wq, wk, wv)):
            nc.sync.dma_start(out=w_rows[:, head, :], in_=w)
        load_x(2)
        v_bias = consts.tile([P, HD], BF16)
        nc.sync.dma_start(out=v_bias[:], in_=bv.partition_broadcast(P))
        head_gain = consts.tile([P, 2, HD], BF16)
        for head, g in enumerate((q_norm_w, k_norm_w)):
            nc.sync.dma_start(out=head_gain[:, head, :], in_=g.partition_broadcast(P))
        for u in range(N_UNITS):
            if u + 3 < N_UNITS:
                load_x(u + 3)
            load_angles(u)

        eps_col = consts.tile([P, 1], F32)
        nc.vector.memset(eps_col[:], EPS)
        first_sqrt = consts.tile([P, 1], F32)
        nc.scalar.activation(out=first_sqrt[:], in_=eps_col[:], func=ACT.Sqrt)
        ident_f32 = consts.tile([P, P], F32)
        make_identity(nc, ident_f32[:])
        ident_bf16 = consts.tile([P, P], BF16)
        make_identity(nc, ident_bf16[:])

        vectorsT_ps = psum.tile([P, P], BF16, tag="back_qk")
        nc.tensor.transpose(vectorsT_ps[:], vector_rows[:], ident_bf16[:])
        vector_cols = consts.tile([P, GAIN_ROWS + 2], F32)
        nc.vector.tensor_copy(out=vector_cols[:], in_=vectorsT_ps[:, 0 : GAIN_ROWS + 2])
        bias_col = vector_cols[:, GAIN_ROWS : GAIN_ROWS + 2]
        ln1_gain = psum.tile([P, HID], F32, bufs=1)
        for c in range(GAIN_ROWS):
            nc.tensor.transpose(
                ln1_gain[:, c * P : (c + 1) * P],
                vector_cols[:, c : c + 1].to_broadcast([P, P]),
                ident_f32[:],
            )

        w_grouped = consts.tile([P, 3, HID], BF16, align_bytes=64)
        w_codes = consts.tile([P, 3 * HD], U32, align_bytes=64)
        w_scales = consts.tile([P, 3 * HD], U8, align_bytes=64)

        def prepare_weights():
            for head in range(3):
                wT_ps = psum.tile([P, 2, HD], F32, tag="back_qk")
                for half in range(2):
                    nc.tensor.transpose(
                        wT_ps[:, half, :],
                        w_rows[:, head, :].bitcast(F32)[:, half * P : (half + 1) * P],
                        ident_f32[:],
                    )
                nc.vector.tensor_copy(
                    out=w_grouped[:, head, :].bitcast(F32).rearrange("p (d h) -> p d h", h=2),
                    in_=wT_ps[:].rearrange("p h d -> p d h"),
                )
            for head in range(3):
                cols = slice(head * HD, (head + 1) * HD)
                nc.vector.quantize_mx(
                    out=w_codes[:, cols].bitcast(FP8X4),
                    scales=w_scales[:, cols],
                    in_=w_grouped[:, head, :],
                )

        x_ss_of, x_std_of, x_rstd_of, h_of, hT_of, grouped_of = {}, {}, {}, {}, {}, {}
        codes_of, scales_of, acc_qk_of, v_ps_of, t1T_of, back_of = {}, {}, {}, {}, {}, {}
        head_ss_of, head_std_of, head_rstd_of, normed_of, cos_ps_of = {}, {}, {}, {}, {}

        def x_sum_of_squares(u):
            x_ss = small.tile([P, TILES], F32)
            for j in range(TILES):
                x_sq = unread.tile([P, HID], BF16)
                nc.scalar.activation(
                    out=x_sq[:], in_=x_of[u][:, j, :], func=ACT.Square,
                    accum_out=x_ss[:, j : j + 1],
                )
            x_ss_of[u] = x_ss

        def x_std(u):
            std = small.tile([P, TILES], F32, name="x_std_sb")
            nc.scalar.activation(
                out=std[:], in_=x_ss_of[u][:], func=ACT.Sqrt, bias=eps_col[:], scale=1.0 / HID
            )
            x_std_of[u] = std

        def x_rstd(u):
            rstd = small.tile([P, TILES], F32, name="x_rstd_sb")
            nc.vector.reciprocal(out=rstd[:], in_=x_std_of[u][:])
            x_rstd_of[u] = rstd

        def first_norm(u):
            h_sb = work.tile([P, TILES, HID], BF16)
            for j in range(TILES):
                nc.vector.scalar_tensor_tensor(
                    out=h_sb[:, j, :], in0=x_of[u][:, j, :], scalar=x_rstd_of[u][:, j : j + 1],
                    in1=ln1_gain[:], op0=ALU.mult, op1=ALU.mult,
                )
            h_of[u] = h_sb

        def h_transposes(u):
            hT_ps = psum.tile([P, TILES, 2, P], F32, bufs=1)
            for j in range(TILES):
                for half in range(2):
                    nc.tensor.transpose(
                        hT_ps[:, j, half, :],
                        h_of[u][:, j, :].bitcast(F32)[:, half * P : (half + 1) * P],
                        ident_f32[:],
                    )
            hT_of[u] = hT_ps

        def h_regroup(u):
            h_grouped = work.tile([P, UNIT * 4], BF16, align_bytes=64)
            nc.scalar.copy(
                out=h_grouped[:].bitcast(F32).rearrange("p (j t h) -> p j t h", j=TILES, h=2),
                in_=hT_of[u][:].rearrange("p j h t -> p j t h"),
            )
            grouped_of[u] = h_grouped

        def h_quantise(u):
            h_codes = work.tile([P, UNIT], U32, align_bytes=64)
            h_scales = work.tile([P, UNIT], U8, align_bytes=64)
            nc.vector.quantize_mx(
                out=h_codes[:].bitcast(FP8X4), scales=h_scales[:], in_=grouped_of[u][:]
            )
            codes_of[u], scales_of[u] = h_codes, h_scales

        def projections(u):
            acc_qk = psum.tile([P, 2, UNIT], F32)
            for head in range(2):
                cols = slice(head * HD, (head + 1) * HD)
                nc.tensor.matmul_mx(
                    out=acc_qk[:, head, :],
                    lhsT=w_codes[:, cols].bitcast(FP8X4), lhsT_scale=w_scales[:, cols],
                    rhs=codes_of[u][:].bitcast(FP8X4), rhs_scale=scales_of[u][:],
                    start=True, stop=True,
                )
            v_ps = psum.tile([P, TILES, HD], F32, bufs=1)
            v_cols = slice(2 * HD, 3 * HD)
            for j in range(TILES):
                tok = slice(j * P, (j + 1) * P)
                nc.tensor.matmul_mx(
                    out=v_ps[:, j, :],
                    lhsT=codes_of[u][:, tok].bitcast(FP8X4), lhsT_scale=scales_of[u][:, tok],
                    rhs=w_codes[:, v_cols].bitcast(FP8X4), rhs_scale=w_scales[:, v_cols],
                    start=True, stop=True,
                )
            acc_qk_of[u], v_ps_of[u] = acc_qk, v_ps

        def finish_v(u):
            v_sb = results.tile([P, TILES, HD], F32)
            nc.vector.tensor_tensor(
                out=v_sb[:], in0=v_ps_of[u][:],
                in1=v_bias[:].unsqueeze(1).to_broadcast([P, TILES, HD]), op=ALU.add,
            )
            nc.sync.dma_start(
                out=v_out[u * UNIT : (u + 1) * UNIT, :].rearrange("(p j) d -> p j d", j=TILES),
                in_=v_sb[:],
            )

        def add_biases(u):
            t1T = work.tile([P, 2, UNIT], F32)
            for head in range(2):
                nc.scalar.activation(
                    out=t1T[:, head, :], in_=acc_qk_of[u][:, head, :], func=ACT.Identity,
                    bias=bias_col[:, head : head + 1],
                )
            t1T_of[u] = t1T

        def turn_back(u):
            back_qk = psum.tile([P, 2, TILES, HD], F32)
            for head in range(2):
                for j in range(TILES):
                    nc.tensor.transpose(
                        back_qk[:, head, j, :], t1T_of[u][:, head, j * P : (j + 1) * P],
                        ident_f32[:],
                    )
            back_of[u] = back_qk

        def head_sums_of_squares(u):
            head_ss = small.tile([P, 2, TILES], F32)
            for head in range(2):
                for j in range(TILES):
                    head_sq = unread.tile([P, HD], BF16)
                    nc.scalar.activation(
                        out=head_sq[:], in_=back_of[u][:, head, j, :], func=ACT.Square,
                        accum_out=head_ss[:, head, j : j + 1],
                    )
            head_ss_of[u] = head_ss

        def head_std(u):
            std = small.tile([P, 2, TILES], F32, name="head_std_sb")
            nc.scalar.activation(
                out=std[:], in_=head_ss_of[u][:], func=ACT.Sqrt, bias=eps_col[:], scale=1.0 / HD
            )
            head_std_of[u] = std

        def head_rstd(u):
            rstd = small.tile([P, 2, TILES], F32, name="head_rstd_sb")
            nc.vector.reciprocal(out=rstd[:], in_=head_std_of[u][:])
            head_rstd_of[u] = rstd

        def head_norm(u):
            normed = work.tile([P, 2, TILES, HD], F32)
            for head in range(2):
                for j in range(TILES):
                    nc.vector.scalar_tensor_tensor(
                        out=normed[:, head, j, :], in0=back_of[u][:, head, j, :],
                        scalar=head_rstd_of[u][:, head, j : j + 1], in1=head_gain[:, head, :],
                        op0=ALU.mult, op1=ALU.mult,
                    )
            normed_of[u] = normed

        def cos_to_psum(u):
            cos_ps = psum.tile([P, TILES, HD], F32, bufs=1)
            nc.tensor.matmul(
                out=cos_ps[:], lhsT=ident_bf16[:], rhs=cos_of[u][:], start=True, stop=True
            )
            cos_ps_of[u] = cos_ps

        def rope(u):
            normed = normed_of[u]
            lo, hi = slice(0, HALF), slice(HALF, HD)
            both = [P, 2, TILES, HD]
            both_half = [P, 2, TILES, HALF]
            crossed = work.tile(both, F32)
            for here, there in ((lo, hi), (hi, lo)):
                nc.gpsimd.tensor_tensor(
                    out=crossed[:, :, :, here], in0=normed[:, :, :, there],
                    in1=sin_of[u][:, :, here].unsqueeze(1).to_broadcast(both_half), op=ALU.mult,
                )
            direct = work.tile(both, F32)
            nc.vector.tensor_tensor(
                out=direct[:], in0=cos_ps_of[u][:].unsqueeze(1).to_broadcast(both), in1=normed[:],
                op=ALU.mult,
            )
            qk_sb = results.tile(both, F32)
            for here, op in ((lo, ALU.subtract), (hi, ALU.add)):
                nc.gpsimd.tensor_tensor(
                    out=qk_sb[:, :, :, here], in0=direct[:, :, :, here],
                    in1=crossed[:, :, :, here], op=op,
                )
            rows = slice(u * UNIT, (u + 1) * UNIT)
            for head, out in enumerate((q_out, k_out)):
                nc.sync.dma_start(
                    out=out[rows, :].rearrange("(p j) d -> p j d", j=TILES),
                    in_=qk_sb[:, head, :, :],
                )

        def live(u):
            return 0 <= u < N_UNITS

        for r in range(N_UNITS + DEPTH):
            if r == WEIGHTS_ROUND:
                prepare_weights()
            if live(r - 5):
                head_sums_of_squares(r - 5)
            if live(r - 1):
                x_rstd(r - 1)
            if live(r - 3):
                h_quantise(r - 3)
            if live(r - 4):
                finish_v(r - 4)
            if live(r - 3):
                projections(r - 3)
            if live(r - 6):
                rope(r - 6)
            if live(r - 5):
                cos_to_psum(r - 5)
            if live(r - 4):
                add_biases(r - 4)
                turn_back(r - 4)
            if live(r - 5):
                head_std(r - 5)
                head_rstd(r - 5)
            if live(r):
                x_sum_of_squares(r)
            if live(r - 2):
                h_regroup(r - 2)
            if live(r):
                x_std(r)
            if live(r - 1):
                first_norm(r - 1)
                h_transposes(r - 1)
            if live(r - 5):
                head_norm(r - 5)
